import numpy as np
import ml_dtypes


def mxq(x, axis, fmt="e4m3"):
    dtype, down = {"e4m3": (ml_dtypes.float8_e4m3fn, 7), "e5m2": (ml_dtypes.float8_e5m2, 14)}[fmt]
    v = np.moveaxis(np.asarray(x, np.float32).astype(ml_dtypes.bfloat16).astype(np.float64), axis, -1)
    blocks = v.reshape(v.shape[:-1] + (-1, 32))
    amax = np.abs(blocks).max(-1, keepdims=True)
    byte = np.maximum(np.where(amax > 0, np.frexp(amax)[1] - 1 + 127, 0) - down, 1)
    scale = np.exp2(byte - 127.0)
    codes = (blocks / scale).astype(np.float32).astype(dtype).astype(np.float64)
    return np.moveaxis((codes * scale).reshape(v.shape), -1, axis)


WIDE = False


def mx_kscale(k):
    if not WIDE:
        return np.ones(k)
    levels = np.array([10, -10, 5, -5, 0])
    a = np.random.permutation(np.resize(levels, k // 512 * 4)).reshape(k // 512, 4)
    idx = np.arange(k)
    return np.exp2(a[idx // 512, idx % 128 // 32])


BF16 = ml_dtypes.bfloat16


def bf(x):
    return np.asarray(x, np.float32).astype(BF16)


def f64(x):
    return np.asarray(x).astype(np.float64)


B, G, DB, DR = 128, 16, 1024, 2048


def mish(v):
    return v * np.tanh(np.log(1.0 + np.exp(v)))


def setup_inputs():
    s, t = mx_kscale(DR), mx_kscale(DB)
    return {"BB_feature": bf(np.random.standard_normal((B, G, DB)) * t),
            "RF_feature": bf(np.random.standard_normal((B, DR)) * s),
            "W_rfrf": bf(np.random.standard_normal((DR, DR)) / np.sqrt(DR) / s),
            "b_rfrf": bf(np.random.standard_normal(DR) * 0.5),
            "W_bbrf": bf(np.random.standard_normal((DR, DB)) * np.sqrt(G / DB) / t),
            "b_bbrf": bf(np.random.standard_normal(DR) * 0.5)}


def reference(BB_feature, RF_feature, W_rfrf, b_rfrf, W_bbrf, b_bbrf):
    BB_mean = np.mean(f64(BB_feature), axis=-2)
    RF_to_RF = mish((mxq(f64(RF_feature), 1, "e4m3") @ mxq(f64(W_rfrf), 1, "e4m3").T) + f64(b_rfrf))
    BB_to_RF = mish((mxq(BB_mean, 1, "e4m3") @ mxq(f64(W_bbrf), 1, "e4m3").T) + f64(b_bbrf))
    return RF_to_RF + BB_to_RF

@@ -1,0 +1,209 @@
+import concourse.mybir as mybir
+from concourse.masks import make_identity
+
+F32 = mybir.dt.float32
+BF16 = mybir.dt.bfloat16
+U32 = mybir.dt.uint32
+U8 = mybir.dt.uint8
+FP8X4 = mybir.dt.float8_e4m3fn_x4
+ACT = mybir.ActivationFunctionType
+ALU = mybir.AluOpType
+
+P = 128
+GROUPS = 16
+D_BB = 1024
+D_RF = 2048
+K_PASS = 512
+ROWS = 2
+WIDTH = P * ROWS
+SLOTS_PER_LAYER = D_RF // WIDTH
+SLOTS = 2 * SLOTS_PER_LAYER
+PIECE = 512
+EXP_CAP = 30.0
+
+FLOPS = 2 * P * D_RF * (D_RF + D_BB)
+
+
+def tile_gnn_layer_pa_kernel(tc, BB_feature, RF_feature, W_rfrf, b_rfrf, W_bbrf, b_bbrf, out):
+    nc = tc.nc
+    with (
+        tc.tile_pool(name="const", bufs=1) as const,
+        tc.tile_pool(name="work", bufs=2) as work,
+        tc.psum_pool(name="tp", bufs=4) as tp,
+        tc.psum_pool(name="accp", bufs=2) as accp,
+        tc.psum_pool(name="meanp", bufs=1) as meanp,
+    ):
+        bias = []
+        for layer, b in enumerate((b_rfrf, b_bbrf)):
+            bias_tile = const.tile([P, D_RF], BF16, name="bias_%d" % layer)
+            nc.scalar.dma_start(out=bias_tile[:], in_=b.partition_broadcast(P))
+            bias.append(bias_tile)
+
+        rf_raw = const.tile([P, D_RF], BF16)
+        nc.sync.dma_start(out=rf_raw[:], in_=RF_feature)
+
+        def load_weight_slot(w, k, index):
+            w_raw = const.tile([P, ROWS * k], BF16, name="w_raw_%d_%d" % (k, index))
+            nc.sync.dma_start(
+                out=w_raw[:],
+                in_=w[index * WIDTH : (index + 1) * WIDTH, :].rearrange("(n j) k -> n (j k)", j=ROWS),
+            )
+            return w_raw
+
+        w_raw_tiles = [load_weight_slot(W_rfrf, D_RF, i) for i in range(SLOTS_PER_LAYER)]
+        bb_rows = BB_feature.rearrange("b g d -> (b g) d")
+        bb_raw_tiles = []
+        for i in range(4):
+            bb_raw = const.tile([P, 4 * D_BB], BF16, name="bb_raw_%d" % i)
+            nc.sync.dma_start(
+                out=bb_raw[:],
+                in_=bb_rows[i * 512 : (i + 1) * 512, :].rearrange("(p e) d -> p (e d)", e=4),
+            )
+            bb_raw_tiles.append(bb_raw)
+        w_raw_tiles.extend([load_weight_slot(W_bbrf, D_BB, i) for i in range(SLOTS_PER_LAYER)])
+
+        ident = const.tile([P, P], F32)
+        make_identity(nc, ident[:])
+        sel_f32 = const.tile([P, 32], F32)
+        nc.vector.tensor_reduce(
+            out=sel_f32[:],
+            in_=ident[:].rearrange("p (n i) -> p n i", i=4),
+            axis=mybir.AxisListType.X,
+            op=ALU.add,
+        )
+        sel = const.tile([P, 32], BF16)
+        nc.vector.tensor_scalar(out=sel[:], in0=sel_f32[:], scalar1=1.0 / GROUPS, scalar2=None, op0=ALU.mult)
+
+        def transpose_and_group(src, rows, k, grouped, first_bank):
+            words = src[:].bitcast(F32)
+            grouped_words = grouped.bitcast(F32).rearrange("p (g n u) -> p g n u", n=P, u=2)
+            n_groups = rows * (k // K_PASS)
+            for pair in range(n_groups // 2):
+                bank = tp.tile([P, 512], F32, tag="tp", name="bank")
+                bank_v = bank[:].rearrange("p (h u n) -> p h u n", h=2, u=2)
+                for h in range(2):
+                    c, j = divmod(2 * pair + h, rows)
+                    for u in range(2):
+                        start_word = j * (k // 2) + 256 * c + 128 * u
+                        nc.tensor.transpose(bank_v[:, h, u, :], words[:, start_word : start_word + P], ident[:])
+                copy = nc.vector.tensor_copy if (first_bank + pair) % 4 == 0 else nc.scalar.copy
+                copy(
+                    out=grouped_words[:, 2 * pair : 2 * pair + 2, :, :],
+                    in_=bank[:].rearrange("p (h u n) -> p h n u", h=2, u=2),
+                )
+
+        def depth_of(slot):
+            return D_RF if slot < SLOTS_PER_LAYER else D_BB
+
+        def transpose_slot(slot):
+            k = depth_of(slot)
+            banks = ROWS * k // K_PASS // 2
+            grouped = work.tile([P, ROWS * D_RF], BF16, align_bytes=64, tag="grouped", name="grouped")
+            transpose_and_group(w_raw_tiles[slot], ROWS, k, grouped[:, : ROWS * k], slot * banks)
+            return grouped
+
+        def quantise_slot(slot, grouped):
+            k = depth_of(slot)
+            codes = work.tile([P, ROWS * D_RF // 4], U32, align_bytes=64, tag="codes", name="codes")
+            scales = work.tile([P, ROWS * D_RF // 4], U8, align_bytes=64, tag="scales", name="scales")
+            n_words = ROWS * k // 4
+            nc.vector.quantize_mx(
+                out=codes[:, :n_words].bitcast(FP8X4), scales=scales[:, :n_words], in_=grouped[:, : ROWS * k]
+            )
+            return codes, scales
+
+        z = [const.tile([P, D_RF], F32, name="z_%d" % layer) for layer in range(2)]
+        soft = [const.tile([P, D_RF], F32, name="soft_%d" % layer) for layer in range(2)]
+        x_grouped = [const.tile([P, k], BF16, align_bytes=64, name="x_grouped_%d" % k) for k in (D_RF, D_BB)]
+        x_codes = [const.tile([P, k // 4], U32, align_bytes=64, name="x_codes_%d" % k) for k in (D_RF, D_BB)]
+        x_scales = [const.tile([P, k // 4], U8, align_bytes=64, name="x_scales_%d" % k) for k in (D_RF, D_BB)]
+
+        def quantise_x(layer):
+            nc.vector.quantize_mx(
+                out=x_codes[layer][:].bitcast(FP8X4), scales=x_scales[layer][:], in_=x_grouped[layer][:]
+            )
+
+        def multiply_slot(slot, w_codes, w_scales):
+            layer = slot // SLOTS_PER_LAYER
+            passes = depth_of(slot) // K_PASS
+            acc = accp.tile([P, WIDTH], F32, tag="acc", name="acc")
+            for c in range(passes):
+                nc.tensor.matmul_mx(
+                    out=acc[:],
+                    lhsT=x_codes[layer][:, c * P : (c + 1) * P].bitcast(FP8X4),
+                    lhsT_scale=x_scales[layer][:, c * P : (c + 1) * P],
+                    rhs=w_codes[:, c * WIDTH : (c + 1) * WIDTH].bitcast(FP8X4),
+                    rhs_scale=w_scales[:, c * WIDTH : (c + 1) * WIDTH],
+                    start=(c == 0),
+                    stop=(c == passes - 1),
+                )
+            return acc
+
+        def add_bias_and_exp(slot, acc):
+            layer = slot // SLOTS_PER_LAYER
+            first = (slot % SLOTS_PER_LAYER) * WIDTH
+            cols = slice(first, first + WIDTH)
+            nc.vector.tensor_tensor(
+                out=z[layer][:, cols].rearrange("p (n j) -> p n j", j=ROWS),
+                in0=acc[:].rearrange("p (j n) -> p n j", j=ROWS),
+                in1=bias[layer][:, cols].rearrange("p (n j) -> p n j", j=ROWS),
+                op=ALU.add,
+            )
+            nc.vector.tensor_scalar(
+                out=soft[layer][:, cols], in0=z[layer][:, cols], scalar1=EXP_CAP, scalar2=None, op0=ALU.min
+            )
+            nc.scalar.activation(out=soft[layer][:, cols], in_=soft[layer][:, cols], func=ACT.Exp)
+
+        def linear_layer(layer):
+            first_slot = layer * SLOTS_PER_LAYER
+            last_slot = first_slot + SLOTS_PER_LAYER - 1
+            grouped = transpose_slot(first_slot)
+            quantise_x(layer)
+            w_codes, w_scales = quantise_slot(first_slot, grouped)
+            acc_before = None
+            for slot in range(first_slot, last_slot + 1):
+                if slot < last_slot:
+                    grouped = transpose_slot(slot + 1)
+                if slot > first_slot:
+                    add_bias_and_exp(slot - 1, acc_before)
+                acc_before = multiply_slot(slot, w_codes, w_scales)
+                if slot < last_slot:
+                    w_codes, w_scales = quantise_slot(slot + 1, grouped)
+            add_bias_and_exp(last_slot, acc_before)
+
+        transpose_and_group(rf_raw, 1, D_RF, x_grouped[0][:], 0)
+        linear_layer(0)
+
+        nc.scalar.activation(out=soft[0][:], in_=soft[0][:], func=ACT.Ln, bias=1.0)
+        nc.scalar.activation(out=soft[0][:], in_=soft[0][:], func=ACT.Tanh)
+        for piece in range(D_RF // PIECE):
+            cols = slice(piece * PIECE, (piece + 1) * PIECE)
+            nc.gpsimd.tensor_tensor(out=soft[0][:, cols], in0=z[0][:, cols], in1=soft[0][:, cols], op=ALU.mult)
+        mean_banks = [meanp.tile([P, 512], F32, tag="mean%d" % c, name="mean%d" % c) for c in range(2)]
+        for i in range(4):
+            bb_v = bb_raw_tiles[i][:].rearrange("p (e c u q w) -> p e c u w q", e=4, c=2, u=2, w=2)
+            for c in range(2):
+                mean_v = mean_banks[c][:].rearrange("p (t b) -> p t b", t=4)
+                for t in range(4):
+                    for e in range(4):
+                        nc.tensor.matmul(
+                            out=mean_v[:, t, 32 * i : 32 * i + 32],
+                            lhsT=bb_v[:, e, c, t // 2, t % 2, :],
+                            rhs=sel[:],
+                            start=(e == 0),
+                            stop=(e == 3),
+                        )
+        for c in range(2):
+            nc.vector.tensor_copy(
+                out=x_grouped[1][:, c * 512 : (c + 1) * 512].rearrange("p (b t) -> p b t", t=4),
+                in_=mean_banks[c][:].rearrange("p (t b) -> p b t", t=4),
+            )
+
+        linear_layer(1)
+        nc.scalar.activation(out=soft[1][:], in_=soft[1][:], func=ACT.Ln, bias=1.0)
+        for piece in range(D_RF // PIECE):
+            cols = slice(piece * PIECE, (piece + 1) * PIECE)
+            nc.scalar.activation(out=soft[1][:, cols], in_=soft[1][:, cols], func=ACT.Tanh)
+            nc.vector.tensor_tensor(out=soft[1][:, cols], in0=z[1][:, cols], in1=soft[1][:, cols], op=ALU.mult)
+            nc.vector.tensor_tensor(out=soft[1][:, cols], in0=soft[1][:, cols], in1=soft[0][:, cols], op=ALU.add)
+            nc.sync.dma_start(out=out[:, cols], in_=soft[1][:, cols])

@@ -19,6 +19,7 @@ WIDTH = P * ROWS
 SLOTS_PER_LAYER = D_RF // WIDTH
 SLOTS = 2 * SLOTS_PER_LAYER
 PIECE = 512
+VECTOR_SLOTS = (11, 12, 13)
 EXP_CAP = 30.0
 
 FLOPS = 2 * P * D_RF * (D_RF + D_BB)
@@ -32,12 +33,12 @@ def tile_gnn_layer_pa_kernel(tc, BB_feature, RF_feature, W_rfrf, b_rfrf, W_bbrf,
         tc.psum_pool(name="tp", bufs=4) as tp,
         tc.psum_pool(name="accp", bufs=2) as accp,
         tc.psum_pool(name="meanp", bufs=1) as meanp,
+        tc.manual_schedule(),
     ):
-        bias = []
-        for layer, b in enumerate((b_rfrf, b_bbrf)):
-            bias_tile = const.tile([P, D_RF], BF16, name="bias_%d" % layer)
-            nc.scalar.dma_start(out=bias_tile[:], in_=b.partition_broadcast(P))
-            bias.append(bias_tile)
+        bias_rows = const.tile([P, P], BF16)
+        nc.vector.memset(bias_rows[:], 0.0)
+        nc.sync.dma_start(out=bias_rows[0:16, :], in_=b_rfrf.rearrange("(r c) -> r c", c=P))
+        nc.sync.dma_start(out=bias_rows[16:32, :], in_=b_bbrf.rearrange("(r c) -> r c", c=P))
 
         rf_raw = const.tile([P, D_RF], BF16)
         nc.sync.dma_start(out=rf_raw[:], in_=RF_feature)
@@ -50,10 +51,12 @@ def tile_gnn_layer_pa_kernel(tc, BB_feature, RF_feature, W_rfrf, b_rfrf, W_bbrf,
             )
             return w_raw
 
-        w_raw_tiles = [load_weight_slot(W_rfrf, D_RF, i) for i in range(SLOTS_PER_LAYER)]
         bb_rows = BB_feature.rearrange("b g d -> (b g) d")
+        w_raw_tiles = []
         bb_raw_tiles = []
         for i in range(4):
+            w_raw_tiles.append(load_weight_slot(W_rfrf, D_RF, 2 * i))
+            w_raw_tiles.append(load_weight_slot(W_rfrf, D_RF, 2 * i + 1))
             bb_raw = const.tile([P, 4 * D_BB], BF16, name="bb_raw_%d" % i)
             nc.sync.dma_start(
                 out=bb_raw[:],
@@ -74,7 +77,7 @@ def tile_gnn_layer_pa_kernel(tc, BB_feature, RF_feature, W_rfrf, b_rfrf, W_bbrf,
         sel = const.tile([P, 32], BF16)
         nc.vector.tensor_scalar(out=sel[:], in0=sel_f32[:], scalar1=1.0 / GROUPS, scalar2=None, op0=ALU.mult)
 
-        def transpose_and_group(src, rows, k, grouped, first_bank):
+        def transpose_and_group(src, rows, k, grouped, vector_banks):
             words = src[:].bitcast(F32)
             grouped_words = grouped.bitcast(F32).rearrange("p (g n u) -> p g n u", n=P, u=2)
             n_groups = rows * (k // K_PASS)
@@ -86,7 +89,7 @@ def tile_gnn_layer_pa_kernel(tc, BB_feature, RF_feature, W_rfrf, b_rfrf, W_bbrf,
                     for u in range(2):
                         start_word = j * (k // 2) + 256 * c + 128 * u
                         nc.tensor.transpose(bank_v[:, h, u, :], words[:, start_word : start_word + P], ident[:])
-                copy = nc.vector.tensor_copy if (first_bank + pair) % 4 == 0 else nc.scalar.copy
+                copy = nc.vector.tensor_copy if pair < vector_banks else nc.scalar.copy
                 copy(
                     out=grouped_words[:, 2 * pair : 2 * pair + 2, :, :],
                     in_=bank[:].rearrange("p (h u n) -> p h n u", h=2, u=2),
@@ -97,9 +100,14 @@ def tile_gnn_layer_pa_kernel(tc, BB_feature, RF_feature, W_rfrf, b_rfrf, W_bbrf,
 
         def transpose_slot(slot):
             k = depth_of(slot)
-            banks = ROWS * k // K_PASS // 2
-            grouped = work.tile([P, ROWS * D_RF], BF16, align_bytes=64, tag="grouped", name="grouped")
-            transpose_and_group(w_raw_tiles[slot], ROWS, k, grouped[:, : ROWS * k], slot * banks)
+            grouped = work.tile([P, ROWS * D_RF], BF16, align_bytes=64, tag="grouped", name="grouped", bufs=3)
+            if slot in VECTOR_SLOTS:
+                vector_banks = 4
+            elif slot < SLOTS_PER_LAYER:
+                vector_banks = 1
+            else:
+                vector_banks = slot % 2
+            transpose_and_group(w_raw_tiles[slot], ROWS, k, grouped[:, : ROWS * k], vector_banks)
             return grouped
 
         def quantise_slot(slot, grouped):
@@ -117,11 +125,30 @@ def tile_gnn_layer_pa_kernel(tc, BB_feature, RF_feature, W_rfrf, b_rfrf, W_bbrf,
         x_grouped = [const.tile([P, k], BF16, align_bytes=64, name="x_grouped_%d" % k) for k in (D_RF, D_BB)]
         x_codes = [const.tile([P, k // 4], U32, align_bytes=64, name="x_codes_%d" % k) for k in (D_RF, D_BB)]
         x_scales = [const.tile([P, k // 4], U8, align_bytes=64, name="x_scales_%d" % k) for k in (D_RF, D_BB)]
+        bias = const.tile([P, 2 * D_RF], F32)
+        mean_banks = [meanp.tile([P, 512], F32, tag="mean%d" % c, name="mean%d" % c) for c in range(2)]
 
         def quantise_x(layer):
             nc.vector.quantize_mx(
                 out=x_codes[layer][:].bitcast(FP8X4), scales=x_scales[layer][:], in_=x_grouped[layer][:]
             )
+
+        def spread_biases():
+            rows_f32 = const.tile([P, P], F32)
+            nc.vector.tensor_copy(out=rows_f32[:], in_=bias_rows[:])
+            columns_bank = tp.tile([P, 512], F32, tag="tp", name="columns_bank")
+            nc.tensor.transpose(columns_bank[:, :P], rows_f32[:], ident[:])
+            columns = const.tile([P, 32], F32)
+            nc.vector.tensor_copy(out=columns[:], in_=columns_bank[:, :32])
+            for index in range(8):
+                bank = tp.tile([P, 512], F32, tag="tp", name="bias_bank")
+                for quarter in range(4):
+                    r = 4 * index + quarter
+                    nc.tensor.transpose(
+                        bank[:, quarter * P : (quarter + 1) * P], columns[:, r : r + 1].to_broadcast([P, P]), ident[:]
+                    )
+                copy = nc.vector.tensor_copy if index % 2 == 0 else nc.scalar.copy
+                copy(out=bias[:, index * 512 : (index + 1) * 512], in_=bank[:])
 
         def multiply_slot(slot, w_codes, w_scales):
             layer = slot // SLOTS_PER_LAYER
@@ -146,7 +173,7 @@ def tile_gnn_layer_pa_kernel(tc, BB_feature, RF_feature, W_rfrf, b_rfrf, W_bbrf,
             nc.vector.tensor_tensor(
                 out=z[layer][:, cols].rearrange("p (n j) -> p n j", j=ROWS),
                 in0=acc[:].rearrange("p (j n) -> p n j", j=ROWS),
-                in1=bias[layer][:, cols].rearrange("p (n j) -> p n j", j=ROWS),
+                in1=bias[:, slot * WIDTH : (slot + 1) * WIDTH].rearrange("p (n j) -> p n j", j=ROWS),
                 op=ALU.add,
             )
             nc.vector.tensor_scalar(
@@ -154,53 +181,53 @@ def tile_gnn_layer_pa_kernel(tc, BB_feature, RF_feature, W_rfrf, b_rfrf, W_bbrf,
             )
             nc.scalar.activation(out=soft[layer][:, cols], in_=soft[layer][:, cols], func=ACT.Exp)
 
-        def linear_layer(layer):
-            first_slot = layer * SLOTS_PER_LAYER
-            last_slot = first_slot + SLOTS_PER_LAYER - 1
-            grouped = transpose_slot(first_slot)
-            quantise_x(layer)
-            w_codes, w_scales = quantise_slot(first_slot, grouped)
-            acc_before = None
-            for slot in range(first_slot, last_slot + 1):
-                if slot < last_slot:
-                    grouped = transpose_slot(slot + 1)
-                if slot > first_slot:
-                    add_bias_and_exp(slot - 1, acc_before)
-                acc_before = multiply_slot(slot, w_codes, w_scales)
-                if slot < last_slot:
-                    w_codes, w_scales = quantise_slot(slot + 1, grouped)
-            add_bias_and_exp(last_slot, acc_before)
-
-        transpose_and_group(rf_raw, 1, D_RF, x_grouped[0][:], 0)
-        linear_layer(0)
-
-        nc.scalar.activation(out=soft[0][:], in_=soft[0][:], func=ACT.Ln, bias=1.0)
-        nc.scalar.activation(out=soft[0][:], in_=soft[0][:], func=ACT.Tanh)
-        for piece in range(D_RF // PIECE):
-            cols = slice(piece * PIECE, (piece + 1) * PIECE)
-            nc.gpsimd.tensor_tensor(out=soft[0][:, cols], in0=z[0][:, cols], in1=soft[0][:, cols], op=ALU.mult)
-        mean_banks = [meanp.tile([P, 512], F32, tag="mean%d" % c, name="mean%d" % c) for c in range(2)]
-        for i in range(4):
+        def mean_part(index):
+            i, c = divmod(index, 2)
             bb_v = bb_raw_tiles[i][:].rearrange("p (e c u q w) -> p e c u w q", e=4, c=2, u=2, w=2)
-            for c in range(2):
-                mean_v = mean_banks[c][:].rearrange("p (t b) -> p t b", t=4)
-                for t in range(4):
-                    for e in range(4):
-                        nc.tensor.matmul(
-                            out=mean_v[:, t, 32 * i : 32 * i + 32],
-                            lhsT=bb_v[:, e, c, t // 2, t % 2, :],
-                            rhs=sel[:],
-                            start=(e == 0),
-                            stop=(e == 3),
-                        )
-        for c in range(2):
-            nc.vector.tensor_copy(
-                out=x_grouped[1][:, c * 512 : (c + 1) * 512].rearrange("p (b t) -> p b t", t=4),
-                in_=mean_banks[c][:].rearrange("p (t b) -> p b t", t=4),
-            )
+            mean_v = mean_banks[c][:].rearrange("p (t b) -> p t b", t=4)
+            for t in range(4):
+                for e in range(4):
+                    nc.tensor.matmul(
+                        out=mean_v[:, t, 32 * i : 32 * i + 32],
+                        lhsT=bb_v[:, e, c, t // 2, t % 2, :],
+                        rhs=sel[:],
+                        start=(e == 0),
+                        stop=(e == 3),
+                    )
 
-        linear_layer(1)
+        transpose_and_group(rf_raw, 1, D_RF, x_grouped[0][:], 1)
+
+        grouped = {}
+        codes = {}
+        acc = {}
+        for step in range(-2, SLOTS + 1):
+            if step + 2 < SLOTS:
+                grouped[step + 2] = transpose_slot(step + 2)
+            if step == -2:
+                quantise_x(0)
+            if step == -1:
+                spread_biases()
+            if step >= 1:
+                add_bias_and_exp(step - 1, acc[step - 1])
+            if step == SLOTS_PER_LAYER:
+                nc.scalar.activation(out=soft[0][:], in_=soft[0][:], func=ACT.Ln, bias=1.0)
+                nc.scalar.activation(out=soft[0][:], in_=soft[0][:], func=ACT.Tanh)
+            if 0 <= step + 1 < SLOTS:
+                codes[step + 1] = quantise_slot(step + 1, grouped[step + 1])
+            if 0 <= step < SLOTS:
+                acc[step] = multiply_slot(step, codes[step][0], codes[step][1])
+            if 0 <= step < SLOTS_PER_LAYER:
+                mean_part(step)
+            if step == SLOTS_PER_LAYER - 1:
+                for c in range(2):
+                    nc.vector.tensor_copy(
+                        out=x_grouped[1][:, c * 512 : (c + 1) * 512].rearrange("p (b t) -> p b t", t=4),
+                        in_=mean_banks[c][:].rearrange("p (t b) -> p b t", t=4),
+                    )
+                quantise_x(1)
+
         nc.scalar.activation(out=soft[1][:], in_=soft[1][:], func=ACT.Ln, bias=1.0)
+        nc.vector.tensor_tensor(out=soft[0][:], in0=z[0][:], in1=soft[0][:], op=ALU.mult)
         for piece in range(D_RF // PIECE):
             cols = slice(piece * PIECE, (piece + 1) * PIECE)
             nc.scalar.activation(out=soft[1][:, cols], in_=soft[1][:, cols], func=ACT.Tanh)

@@ -18,8 +18,7 @@ ROWS = 2
 WIDTH = P * ROWS
 SLOTS_PER_LAYER = D_RF // WIDTH
 SLOTS = 2 * SLOTS_PER_LAYER
-PIECE = 512
-VECTOR_SLOTS = (11, 12, 13)
+FIRST_BATCH = 11
 EXP_CAP = 30.0
 
 FLOPS = 2 * P * D_RF * (D_RF + D_BB)
@@ -101,7 +100,7 @@ def tile_gnn_layer_pa_kernel(tc, BB_feature, RF_feature, W_rfrf, b_rfrf, W_bbrf,
         def transpose_slot(slot):
             k = depth_of(slot)
             grouped = work.tile([P, ROWS * D_RF], BF16, align_bytes=64, tag="grouped", name="grouped", bufs=3)
-            if slot in VECTOR_SLOTS:
+            if slot >= FIRST_BATCH + 3:
                 vector_banks = 4
             elif slot < SLOTS_PER_LAYER:
                 vector_banks = 1
@@ -120,8 +119,8 @@ def tile_gnn_layer_pa_kernel(tc, BB_feature, RF_feature, W_rfrf, b_rfrf, W_bbrf,
             )
             return codes, scales
 
-        z = [const.tile([P, D_RF], F32, name="z_%d" % layer) for layer in range(2)]
-        soft = [const.tile([P, D_RF], F32, name="soft_%d" % layer) for layer in range(2)]
+        z = const.tile([P, 2 * D_RF], F32)
+        soft = const.tile([P, 2 * D_RF], F32)
         x_grouped = [const.tile([P, k], BF16, align_bytes=64, name="x_grouped_%d" % k) for k in (D_RF, D_BB)]
         x_codes = [const.tile([P, k // 4], U32, align_bytes=64, name="x_codes_%d" % k) for k in (D_RF, D_BB)]
         x_scales = [const.tile([P, k // 4], U8, align_bytes=64, name="x_scales_%d" % k) for k in (D_RF, D_BB)]
@@ -167,19 +166,15 @@ def tile_gnn_layer_pa_kernel(tc, BB_feature, RF_feature, W_rfrf, b_rfrf, W_bbrf,
             return acc
 
         def add_bias_and_exp(slot, acc):
-            layer = slot // SLOTS_PER_LAYER
-            first = (slot % SLOTS_PER_LAYER) * WIDTH
-            cols = slice(first, first + WIDTH)
+            cols = slice(slot * WIDTH, (slot + 1) * WIDTH)
             nc.vector.tensor_tensor(
-                out=z[layer][:, cols].rearrange("p (n j) -> p n j", j=ROWS),
+                out=z[:, cols].rearrange("p (n j) -> p n j", j=ROWS),
                 in0=acc[:].rearrange("p (j n) -> p n j", j=ROWS),
-                in1=bias[:, slot * WIDTH : (slot + 1) * WIDTH].rearrange("p (n j) -> p n j", j=ROWS),
+                in1=bias[:, cols].rearrange("p (n j) -> p n j", j=ROWS),
                 op=ALU.add,
             )
-            nc.vector.tensor_scalar(
-                out=soft[layer][:, cols], in0=z[layer][:, cols], scalar1=EXP_CAP, scalar2=None, op0=ALU.min
-            )
-            nc.scalar.activation(out=soft[layer][:, cols], in_=soft[layer][:, cols], func=ACT.Exp)
+            nc.vector.tensor_scalar(out=soft[:, cols], in0=z[:, cols], scalar1=EXP_CAP, scalar2=None, op0=ALU.min)
+            nc.scalar.activation(out=soft[:, cols], in_=soft[:, cols], func=ACT.Exp)
 
         def mean_part(index):
             i, c = divmod(index, 2)
@@ -197,6 +192,8 @@ def tile_gnn_layer_pa_kernel(tc, BB_feature, RF_feature, W_rfrf, b_rfrf, W_bbrf,
 
         transpose_and_group(rf_raw, 1, D_RF, x_grouped[0][:], 1)
 
+        early = slice(0, FIRST_BATCH * WIDTH)
+        late = slice(FIRST_BATCH * WIDTH, SLOTS * WIDTH)
         grouped = {}
         codes = {}
         acc = {}
@@ -209,9 +206,9 @@ def tile_gnn_layer_pa_kernel(tc, BB_feature, RF_feature, W_rfrf, b_rfrf, W_bbrf,
                 spread_biases()
             if step >= 1:
                 add_bias_and_exp(step - 1, acc[step - 1])
-            if step == SLOTS_PER_LAYER:
-                nc.scalar.activation(out=soft[0][:], in_=soft[0][:], func=ACT.Ln, bias=1.0)
-                nc.scalar.activation(out=soft[0][:], in_=soft[0][:], func=ACT.Tanh)
+            if step == FIRST_BATCH:
+                nc.scalar.activation(out=soft[:, early], in_=soft[:, early], func=ACT.Ln, bias=1.0)
+                nc.scalar.activation(out=soft[:, early], in_=soft[:, early], func=ACT.Tanh)
             if 0 <= step + 1 < SLOTS:
                 codes[step + 1] = quantise_slot(step + 1, grouped[step + 1])
             if 0 <= step < SLOTS:
@@ -226,11 +223,13 @@ def tile_gnn_layer_pa_kernel(tc, BB_feature, RF_feature, W_rfrf, b_rfrf, W_bbrf,
                     )
                 quantise_x(1)
 
-        nc.scalar.activation(out=soft[1][:], in_=soft[1][:], func=ACT.Ln, bias=1.0)
-        nc.vector.tensor_tensor(out=soft[0][:], in0=z[0][:], in1=soft[0][:], op=ALU.mult)
-        for piece in range(D_RF // PIECE):
-            cols = slice(piece * PIECE, (piece + 1) * PIECE)
-            nc.scalar.activation(out=soft[1][:, cols], in_=soft[1][:, cols], func=ACT.Tanh)
-            nc.vector.tensor_tensor(out=soft[1][:, cols], in0=z[1][:, cols], in1=soft[1][:, cols], op=ALU.mult)
-            nc.vector.tensor_tensor(out=soft[1][:, cols], in0=soft[1][:, cols], in1=soft[0][:, cols], op=ALU.add)
-            nc.sync.dma_start(out=out[:, cols], in_=soft[1][:, cols])
+        nc.scalar.activation(out=soft[:, late], in_=soft[:, late], func=ACT.Ln, bias=1.0)
+        nc.vector.tensor_tensor(out=soft[:, early], in0=z[:, early], in1=soft[:, early], op=ALU.mult)
+        for slot in range(SLOTS_PER_LAYER, SLOTS):
+            cols = slice(slot * WIDTH, (slot + 1) * WIDTH)
+            out_cols = slice((slot - SLOTS_PER_LAYER) * WIDTH, (slot - SLOTS_PER_LAYER + 1) * WIDTH)
+            if slot >= FIRST_BATCH:
+                nc.scalar.activation(out=soft[:, cols], in_=soft[:, cols], func=ACT.Tanh)
+                nc.vector.tensor_tensor(out=soft[:, cols], in0=z[:, cols], in1=soft[:, cols], op=ALU.mult)
+            nc.vector.tensor_tensor(out=soft[:, cols], in0=soft[:, cols], in1=soft[:, out_cols], op=ALU.add)
+            nc.sync.dma_start(out=out[:, out_cols], in_=soft[:, cols])

@@ -18,7 +18,6 @@ ROWS = 2
 WIDTH = P * ROWS
 SLOTS_PER_LAYER = D_RF // WIDTH
 SLOTS = 2 * SLOTS_PER_LAYER
-FIRST_BATCH = 11
 EXP_CAP = 30.0
 
 FLOPS = 2 * P * D_RF * (D_RF + D_BB)
@@ -50,12 +49,10 @@ def tile_gnn_layer_pa_kernel(tc, BB_feature, RF_feature, W_rfrf, b_rfrf, W_bbrf,
             )
             return w_raw
 
+        w_raw_tiles = [load_weight_slot(W_rfrf, D_RF, i) for i in range(SLOTS_PER_LAYER)]
         bb_rows = BB_feature.rearrange("b g d -> (b g) d")
-        w_raw_tiles = []
         bb_raw_tiles = []
         for i in range(4):
-            w_raw_tiles.append(load_weight_slot(W_rfrf, D_RF, 2 * i))
-            w_raw_tiles.append(load_weight_slot(W_rfrf, D_RF, 2 * i + 1))
             bb_raw = const.tile([P, 4 * D_BB], BF16, name="bb_raw_%d" % i)
             nc.sync.dma_start(
                 out=bb_raw[:],
@@ -100,12 +97,7 @@ def tile_gnn_layer_pa_kernel(tc, BB_feature, RF_feature, W_rfrf, b_rfrf, W_bbrf,
         def transpose_slot(slot):
             k = depth_of(slot)
             grouped = work.tile([P, ROWS * D_RF], BF16, align_bytes=64, tag="grouped", name="grouped", bufs=3)
-            if slot >= FIRST_BATCH + 3:
-                vector_banks = 4
-            elif slot < SLOTS_PER_LAYER:
-                vector_banks = 1
-            else:
-                vector_banks = slot % 2
+            vector_banks = 1 if slot < SLOTS_PER_LAYER else 0
             transpose_and_group(w_raw_tiles[slot], ROWS, k, grouped[:, : ROWS * k], vector_banks)
             return grouped
 
@@ -176,60 +168,64 @@ def tile_gnn_layer_pa_kernel(tc, BB_feature, RF_feature, W_rfrf, b_rfrf, W_bbrf,
             nc.vector.tensor_scalar(out=soft[:, cols], in0=z[:, cols], scalar1=EXP_CAP, scalar2=None, op0=ALU.min)
             nc.scalar.activation(out=soft[:, cols], in_=soft[:, cols], func=ACT.Exp)
 
-        def mean_part(index):
-            i, c = divmod(index, 2)
+        def mean_chunk(i):
             bb_v = bb_raw_tiles[i][:].rearrange("p (e c u q w) -> p e c u w q", e=4, c=2, u=2, w=2)
-            mean_v = mean_banks[c][:].rearrange("p (t b) -> p t b", t=4)
-            for t in range(4):
-                for e in range(4):
-                    nc.tensor.matmul(
-                        out=mean_v[:, t, 32 * i : 32 * i + 32],
-                        lhsT=bb_v[:, e, c, t // 2, t % 2, :],
-                        rhs=sel[:],
-                        start=(e == 0),
-                        stop=(e == 3),
-                    )
+            for c in range(2):
+                mean_v = mean_banks[c][:].rearrange("p (t b) -> p t b", t=4)
+                for t in range(4):
+                    for e in range(4):
+                        nc.tensor.matmul(
+                            out=mean_v[:, t, 32 * i : 32 * i + 32],
+                            lhsT=bb_v[:, e, c, t // 2, t % 2, :],
+                            rhs=sel[:],
+                            start=(e == 0),
+                            stop=(e == 3),
+                        )
 
+        def linear_layer(layer):
+            first = layer * SLOTS_PER_LAYER
+            grouped = {}
+            codes = {}
+            acc = {}
+            for step in range(-2, SLOTS_PER_LAYER + 1):
+                slot = first + step
+                if step + 2 < SLOTS_PER_LAYER:
+                    grouped[slot + 2] = transpose_slot(slot + 2)
+                if step == -2:
+                    quantise_x(layer)
+                if step >= 1:
+                    add_bias_and_exp(slot - 1, acc[slot - 1])
+                if 0 <= step + 1 < SLOTS_PER_LAYER:
+                    codes[slot + 1] = quantise_slot(slot + 1, grouped[slot + 1])
+                if 0 <= step < SLOTS_PER_LAYER:
+                    acc[slot] = multiply_slot(slot, codes[slot][0], codes[slot][1])
+
+        layer_cols = [slice(layer * D_RF, (layer + 1) * D_RF) for layer in range(2)]
+
+        spread_biases()
         transpose_and_group(rf_raw, 1, D_RF, x_grouped[0][:], 1)
+        linear_layer(0)
 
-        early = slice(0, FIRST_BATCH * WIDTH)
-        late = slice(FIRST_BATCH * WIDTH, SLOTS * WIDTH)
-        grouped = {}
-        codes = {}
-        acc = {}
-        for step in range(-2, SLOTS + 1):
-            if step + 2 < SLOTS:
-                grouped[step + 2] = transpose_slot(step + 2)
-            if step == -2:
-                quantise_x(0)
-            if step == -1:
-                spread_biases()
-            if step >= 1:
-                add_bias_and_exp(step - 1, acc[step - 1])
-            if step == FIRST_BATCH:
-                nc.scalar.activation(out=soft[:, early], in_=soft[:, early], func=ACT.Ln, bias=1.0)
-                nc.scalar.activation(out=soft[:, early], in_=soft[:, early], func=ACT.Tanh)
-            if 0 <= step + 1 < SLOTS:
-                codes[step + 1] = quantise_slot(step + 1, grouped[step + 1])
-            if 0 <= step < SLOTS:
-                acc[step] = multiply_slot(step, codes[step][0], codes[step][1])
-            if 0 <= step < SLOTS_PER_LAYER:
-                mean_part(step)
-            if step == SLOTS_PER_LAYER - 1:
-                for c in range(2):
-                    nc.vector.tensor_copy(
-                        out=x_grouped[1][:, c * 512 : (c + 1) * 512].rearrange("p (b t) -> p b t", t=4),
-                        in_=mean_banks[c][:].rearrange("p (t b) -> p b t", t=4),
-                    )
-                quantise_x(1)
+        nc.scalar.activation(out=soft[:, layer_cols[0]], in_=soft[:, layer_cols[0]], func=ACT.Ln, bias=1.0)
+        nc.scalar.activation(out=soft[:, layer_cols[0]], in_=soft[:, layer_cols[0]], func=ACT.Tanh)
+        for i in range(4):
+            mean_chunk(i)
+        for c in range(2):
+            nc.vector.tensor_copy(
+                out=x_grouped[1][:, c * 512 : (c + 1) * 512].rearrange("p (b t) -> p b t", t=4),
+                in_=mean_banks[c][:].rearrange("p (t b) -> p b t", t=4),
+            )
 
-        nc.scalar.activation(out=soft[:, late], in_=soft[:, late], func=ACT.Ln, bias=1.0)
-        nc.vector.tensor_tensor(out=soft[:, early], in0=z[:, early], in1=soft[:, early], op=ALU.mult)
+        linear_layer(1)
+
+        nc.scalar.activation(out=soft[:, layer_cols[1]], in_=soft[:, layer_cols[1]], func=ACT.Ln, bias=1.0)
+        nc.vector.tensor_tensor(
+            out=soft[:, layer_cols[0]], in0=z[:, layer_cols[0]], in1=soft[:, layer_cols[0]], op=ALU.mult
+        )
         for slot in range(SLOTS_PER_LAYER, SLOTS):
             cols = slice(slot * WIDTH, (slot + 1) * WIDTH)
             out_cols = slice((slot - SLOTS_PER_LAYER) * WIDTH, (slot - SLOTS_PER_LAYER + 1) * WIDTH)
-            if slot >= FIRST_BATCH:
-                nc.scalar.activation(out=soft[:, cols], in_=soft[:, cols], func=ACT.Tanh)
-                nc.vector.tensor_tensor(out=soft[:, cols], in0=z[:, cols], in1=soft[:, cols], op=ALU.mult)
+            nc.scalar.activation(out=soft[:, cols], in_=soft[:, cols], func=ACT.Tanh)
+            nc.vector.tensor_tensor(out=soft[:, cols], in0=z[:, cols], in1=soft[:, cols], op=ALU.mult)
             nc.vector.tensor_tensor(out=soft[:, cols], in0=soft[:, cols], in1=soft[:, out_cols], op=ALU.add)
             nc.sync.dma_start(out=out[:, out_cols], in_=soft[:, cols])

import concourse.mybir as mybir
from concourse.masks import make_identity

F32 = mybir.dt.float32
BF16 = mybir.dt.bfloat16
U32 = mybir.dt.uint32
U8 = mybir.dt.uint8
FP8X4 = mybir.dt.float8_e4m3fn_x4
ACT = mybir.ActivationFunctionType
ALU = mybir.AluOpType

P = 128
GROUPS = 16
D_BB = 1024
D_RF = 2048
K_PASS = 512
ROWS = 2
WIDTH = P * ROWS
SLOTS_PER_LAYER = D_RF // WIDTH
SLOTS = 2 * SLOTS_PER_LAYER
EXP_CAP = 30.0

FLOPS = 2 * P * D_RF * (D_RF + D_BB)


def tile_gnn_layer_pa_kernel(tc, BB_feature, RF_feature, W_rfrf, b_rfrf, W_bbrf, b_bbrf, out):
    nc = tc.nc
    with (
        tc.tile_pool(name="const", bufs=1) as const,
        tc.tile_pool(name="work", bufs=2) as work,
        tc.psum_pool(name="tp", bufs=4) as tp,
        tc.psum_pool(name="accp", bufs=2) as accp,
        tc.psum_pool(name="meanp", bufs=1) as meanp,
        tc.manual_schedule(),
    ):
        bias_rows = const.tile([P, P], BF16)
        nc.vector.memset(bias_rows[:], 0.0)
        nc.sync.dma_start(out=bias_rows[0:16, :], in_=b_rfrf.rearrange("(r c) -> r c", c=P))
        nc.sync.dma_start(out=bias_rows[16:32, :], in_=b_bbrf.rearrange("(r c) -> r c", c=P))

        rf_raw = const.tile([P, D_RF], BF16)
        nc.sync.dma_start(out=rf_raw[:], in_=RF_feature)

        def load_weight_slot(w, k, index):
            w_raw = const.tile([P, ROWS * k], BF16, name="w_raw_%d_%d" % (k, index))
            nc.sync.dma_start(
                out=w_raw[:],
                in_=w[index * WIDTH : (index + 1) * WIDTH, :].rearrange("(n j) k -> n (j k)", j=ROWS),
            )
            return w_raw

        w_raw_tiles = [load_weight_slot(W_rfrf, D_RF, i) for i in range(SLOTS_PER_LAYER)]
        bb_rows = BB_feature.rearrange("b g d -> (b g) d")
        bb_raw_tiles = []
        for i in range(4):
            bb_raw = const.tile([P, 4 * D_BB], BF16, name="bb_raw_%d" % i)
            nc.sync.dma_start(
                out=bb_raw[:],
                in_=bb_rows[i * 512 : (i + 1) * 512, :].rearrange("(p e) d -> p (e d)", e=4),
            )
            bb_raw_tiles.append(bb_raw)
        w_raw_tiles.extend([load_weight_slot(W_bbrf, D_BB, i) for i in range(SLOTS_PER_LAYER)])

        ident = const.tile([P, P], F32)
        make_identity(nc, ident[:])
        sel_f32 = const.tile([P, 32], F32)
        nc.vector.tensor_reduce(
            out=sel_f32[:],
            in_=ident[:].rearrange("p (n i) -> p n i", i=4),
            axis=mybir.AxisListType.X,
            op=ALU.add,
        )
        sel = const.tile([P, 32], BF16)
        nc.vector.tensor_scalar(out=sel[:], in0=sel_f32[:], scalar1=1.0 / GROUPS, scalar2=None, op0=ALU.mult)

        def transpose_and_group(src, rows, k, grouped, vector_banks):
            words = src[:].bitcast(F32)
            grouped_words = grouped.bitcast(F32).rearrange("p (g n u) -> p g n u", n=P, u=2)
            n_groups = rows * (k // K_PASS)
            for pair in range(n_groups // 2):
                bank = tp.tile([P, 512], F32, tag="tp", name="bank")
                bank_v = bank[:].rearrange("p (h u n) -> p h u n", h=2, u=2)
                for h in range(2):
                    c, j = divmod(2 * pair + h, rows)
                    for u in range(2):
                        start_word = j * (k // 2) + 256 * c + 128 * u
                        nc.tensor.transpose(bank_v[:, h, u, :], words[:, start_word : start_word + P], ident[:])
                copy = nc.vector.tensor_copy if pair < vector_banks else nc.scalar.copy
                copy(
                    out=grouped_words[:, 2 * pair : 2 * pair + 2, :, :],
                    in_=bank[:].rearrange("p (h u n) -> p h n u", h=2, u=2),
                )

        def depth_of(slot):
            return D_RF if slot < SLOTS_PER_LAYER else D_BB

        def transpose_slot(slot):
            k = depth_of(slot)
            grouped = work.tile([P, ROWS * D_RF], BF16, align_bytes=64, tag="grouped", name="grouped", bufs=3)
            vector_banks = 1 if slot < SLOTS_PER_LAYER else 0
            transpose_and_group(w_raw_tiles[slot], ROWS, k, grouped[:, : ROWS * k], vector_banks)
            return grouped

        def quantise_slot(slot, grouped):
            k = depth_of(slot)
            codes = work.tile([P, ROWS * D_RF // 4], U32, align_bytes=64, tag="codes", name="codes")
            scales = work.tile([P, ROWS * D_RF // 4], U8, align_bytes=64, tag="scales", name="scales")
            n_words = ROWS * k // 4
            nc.vector.quantize_mx(
                out=codes[:, :n_words].bitcast(FP8X4), scales=scales[:, :n_words], in_=grouped[:, : ROWS * k]
            )
            return codes, scales

        z = const.tile([P, 2 * D_RF], F32)
        soft = const.tile([P, 2 * D_RF], F32)
        x_grouped = [const.tile([P, k], BF16, align_bytes=64, name="x_grouped_%d" % k) for k in (D_RF, D_BB)]
        x_codes = [const.tile([P, k // 4], U32, align_bytes=64, name="x_codes_%d" % k) for k in (D_RF, D_BB)]
        x_scales = [const.tile([P, k // 4], U8, align_bytes=64, name="x_scales_%d" % k) for k in (D_RF, D_BB)]
        bias = const.tile([P, 2 * D_RF], F32)
        mean_banks = [meanp.tile([P, 512], F32, tag="mean%d" % c, name="mean%d" % c) for c in range(2)]

        def quantise_x(layer):
            nc.vector.quantize_mx(
                out=x_codes[layer][:].bitcast(FP8X4), scales=x_scales[layer][:], in_=x_grouped[layer][:]
            )

        def spread_biases():
            rows_f32 = const.tile([P, P], F32)
            nc.vector.tensor_copy(out=rows_f32[:], in_=bias_rows[:])
            columns_bank = tp.tile([P, 512], F32, tag="tp", name="columns_bank")
            nc.tensor.transpose(columns_bank[:, :P], rows_f32[:], ident[:])
            columns = const.tile([P, 32], F32)
            nc.vector.tensor_copy(out=columns[:], in_=columns_bank[:, :32])
            for index in range(8):
                bank = tp.tile([P, 512], F32, tag="tp", name="bias_bank")
                for quarter in range(4):
                    r = 4 * index + quarter
                    nc.tensor.transpose(
                        bank[:, quarter * P : (quarter + 1) * P], columns[:, r : r + 1].to_broadcast([P, P]), ident[:]
                    )
                copy = nc.vector.tensor_copy if index % 2 == 0 else nc.scalar.copy
                copy(out=bias[:, index * 512 : (index + 1) * 512], in_=bank[:])

        def multiply_slot(slot, w_codes, w_scales):
            layer = slot // SLOTS_PER_LAYER
            passes = depth_of(slot) // K_PASS
            acc = accp.tile([P, WIDTH], F32, tag="acc", name="acc")
            for c in range(passes):
                nc.tensor.matmul_mx(
                    out=acc[:],
                    lhsT=x_codes[layer][:, c * P : (c + 1) * P].bitcast(FP8X4),
                    lhsT_scale=x_scales[layer][:, c * P : (c + 1) * P],
                    rhs=w_codes[:, c * WIDTH : (c + 1) * WIDTH].bitcast(FP8X4),
                    rhs_scale=w_scales[:, c * WIDTH : (c + 1) * WIDTH],
                    start=(c == 0),
                    stop=(c == passes - 1),
                )
            return acc

        def add_bias_and_exp(slot, acc):
            cols = slice(slot * WIDTH, (slot + 1) * WIDTH)
            nc.vector.tensor_tensor(
                out=z[:, cols].rearrange("p (n j) -> p n j", j=ROWS),
                in0=acc[:].rearrange("p (j n) -> p n j", j=ROWS),
                in1=bias[:, cols].rearrange("p (n j) -> p n j", j=ROWS),
                op=ALU.add,
            )
            nc.vector.tensor_scalar(out=soft[:, cols], in0=z[:, cols], scalar1=EXP_CAP, scalar2=None, op0=ALU.min)
            nc.scalar.activation(out=soft[:, cols], in_=soft[:, cols], func=ACT.Exp)

        def mean_chunk(i):
            bb_v = bb_raw_tiles[i][:].rearrange("p (e c u q w) -> p e c u w q", e=4, c=2, u=2, w=2)
            for c in range(2):
                mean_v = mean_banks[c][:].rearrange("p (t b) -> p t b", t=4)
                for t in range(4):
                    for e in range(4):
                        nc.tensor.matmul(
                            out=mean_v[:, t, 32 * i : 32 * i + 32],
                            lhsT=bb_v[:, e, c, t // 2, t % 2, :],
                            rhs=sel[:],
                            start=(e == 0),
                            stop=(e == 3),
                        )

        def linear_layer(layer):
            first = layer * SLOTS_PER_LAYER
            grouped = {}
            codes = {}
            acc = {}
            for step in range(-2, SLOTS_PER_LAYER + 1):
                slot = first + step
                if step + 2 < SLOTS_PER_LAYER:
                    grouped[slot + 2] = transpose_slot(slot + 2)
                if step == -2:
                    quantise_x(layer)
                if step >= 1:
                    add_bias_and_exp(slot - 1, acc[slot - 1])
                if 0 <= step + 1 < SLOTS_PER_LAYER:
                    codes[slot + 1] = quantise_slot(slot + 1, grouped[slot + 1])
                if 0 <= step < SLOTS_PER_LAYER:
                    acc[slot] = multiply_slot(slot, codes[slot][0], codes[slot][1])

        layer_cols = [slice(layer * D_RF, (layer + 1) * D_RF) for layer in range(2)]

        spread_biases()
        transpose_and_group(rf_raw, 1, D_RF, x_grouped[0][:], 1)
        linear_layer(0)

        nc.scalar.activation(out=soft[:, layer_cols[0]], in_=soft[:, layer_cols[0]], func=ACT.Ln, bias=1.0)
        nc.scalar.activation(out=soft[:, layer_cols[0]], in_=soft[:, layer_cols[0]], func=ACT.Tanh)
        for i in range(4):
            mean_chunk(i)
        for c in range(2):
            nc.vector.tensor_copy(
                out=x_grouped[1][:, c * 512 : (c + 1) * 512].rearrange("p (b t) -> p b t", t=4),
                in_=mean_banks[c][:].rearrange("p (t b) -> p b t", t=4),
            )

        linear_layer(1)

        nc.scalar.activation(out=soft[:, layer_cols[1]], in_=soft[:, layer_cols[1]], func=ACT.Ln, bias=1.0)
        nc.vector.tensor_tensor(
            out=soft[:, layer_cols[0]], in0=z[:, layer_cols[0]], in1=soft[:, layer_cols[0]], op=ALU.mult
        )
        for slot in range(SLOTS_PER_LAYER, SLOTS):
            cols = slice(slot * WIDTH, (slot + 1) * WIDTH)
            out_cols = slice((slot - SLOTS_PER_LAYER) * WIDTH, (slot - SLOTS_PER_LAYER + 1) * WIDTH)
            nc.scalar.activation(out=soft[:, cols], in_=soft[:, cols], func=ACT.Tanh)
            nc.vector.tensor_tensor(out=soft[:, cols], in0=z[:, cols], in1=soft[:, cols], op=ALU.mult)
            nc.vector.tensor_tensor(out=soft[:, cols], in0=soft[:, cols], in1=soft[:, out_cols], op=ALU.add)
            nc.sync.dma_start(out=out[:, out_cols], in_=soft[:, cols])
